import numpy as np
import ml_dtypes


def mxq(x, axis, fmt="e4m3"):
    dtype, down = {"e4m3": (ml_dtypes.float8_e4m3fn, 7), "e5m2": (ml_dtypes.float8_e5m2, 14)}[fmt]
    v = np.moveaxis(np.asarray(x, np.float32).astype(ml_dtypes.bfloat16).astype(np.float64), axis, -1)
    blocks = v.reshape(v.shape[:-1] + (-1, 32))
    amax = np.abs(blocks).max(-1, keepdims=True)
    byte = np.maximum(np.where(amax > 0, np.frexp(amax)[1] - 1 + 127, 0) - down, 1)
    scale = np.exp2(byte - 127.0)
    codes = (blocks / scale).astype(np.float32).astype(dtype).astype(np.float64)
    return np.moveaxis((codes * scale).reshape(v.shape), -1, axis)


WIDE = False


def mx_kscale(k):
    if not WIDE:
        return np.ones(k)
    levels = np.array([10, -10, 5, -5, 0])
    if k % 512:
        return np.exp2(np.random.permutation(np.resize(levels, k // 32))).repeat(32)
    a = np.empty((k // 512, 16))
    for p in range(k // 512):
        a[p, :8] = np.random.permutation(np.resize(levels, 8))
        for g in range(8):
            far = levels[np.abs(levels - a[p, g]) >= 10]
            a[p, g + 8] = far[np.random.randint(len(far))]
    return np.exp2(a.ravel()).repeat(32)


BF16 = ml_dtypes.bfloat16


def bf(x):
    return np.asarray(x, np.float32).astype(BF16)


def f64(x):
    return np.asarray(x).astype(np.float64)


B, IDIM, HDIM, ODIM, S, DEPTH, NACT, NTOP = 4096, 1024, 512, 512, 128, 32, 3, 2


def sigmoid(v):
    return 1.0 / (1.0 + np.exp(-v))


def setup_inputs():
    s, t = mx_kscale(IDIM), mx_kscale(HDIM)
    return {"x": bf(np.random.standard_normal((B, IDIM)) * s),
            "hidden": bf(np.random.standard_normal((B, HDIM)) * t),
            "stack_top": bf(np.random.standard_normal((B, NTOP, S))),
            "Wi": bf(np.random.standard_normal((HDIM, IDIM)) * 0.7 / np.sqrt(IDIM) / s),
            "bi": bf(np.random.standard_normal(HDIM) * 0.2),
            "Wh": bf(np.random.standard_normal((HDIM, HDIM)) * 0.7 / np.sqrt(HDIM) / t),
            "bh": bf(np.random.standard_normal(HDIM) * 0.2),
            "W0": bf(np.random.standard_normal((HDIM, S)) * 0.5 / np.sqrt(S)),
            "b0": bf(np.random.standard_normal(HDIM) * 0.2),
            "W1": bf(np.random.standard_normal((HDIM, S)) * 0.5 / np.sqrt(S)),
            "b1": bf(np.random.standard_normal(HDIM) * 0.2)}


def reference(x, hidden, stack_top, Wi, bi, Wh, bh, W0, b0, W1, b1):
    pre = ((mxq(f64(x), 1, "e4m3") @ mxq(f64(Wi), 1, "e4m3").T) + f64(bi)
           + (mxq(f64(hidden), 1, "e4m3") @ mxq(f64(Wh), 1, "e4m3").T) + f64(bh)
           + f64(stack_top)[:, 0] @ f64(W0).T + f64(b0)
           + f64(stack_top)[:, 1] @ f64(W1).T + f64(b1))
    return sigmoid(pre)

@@ -1,0 +1,298 @@
+from contextlib import ExitStack
+
+import concourse.masks as masks
+import concourse.mybir as mybir
+
+F32 = mybir.dt.float32
+BF16 = mybir.dt.bfloat16
+U32 = mybir.dt.uint32
+U8 = mybir.dt.uint8
+FP8X4 = mybir.dt.float8_e4m3fn_x4
+ADD = mybir.AluOpType.add
+SIGMOID = mybir.ActivationFunctionType.Sigmoid
+
+P = 128
+B, IDIM, HDIM, SK = 4096, 1024, 512, 256
+NT = B // P
+G = 2
+NG = NT // G
+FLOPS = 2 * B * HDIM * (IDIM + HDIM + SK)
+
+CHUNKS = (2, 2, 2, 2, 4, 4, 4, 4, 4, 4)
+LOOKAHEAD = 6
+WEAVE = 2
+OBUFS = 8
+
+
+def tile_stackrnn_pa_t_kernel(tc, x, hidden, stack_top, Wi, bi, Wh, bh, W0, b0, W1, b1, out):
+    nc = tc.nc
+    x_v = x.rearrange("(p t) k -> p t k", t=NT)
+    h_v = hidden.rearrange("(p t) k -> p t k", t=NT)
+    s_v = stack_top.rearrange("(p t) s k -> p t (s k)", t=NT)
+    o_v = out.rearrange("(p t) h -> p t h", t=NT)
+
+    with ExitStack() as ctx:
+        const = ctx.enter_context(tc.tile_pool(name="const", bufs=1))
+        inp = ctx.enter_context(tc.tile_pool(name="inp", bufs=1))
+        work = ctx.enter_context(tc.tile_pool(name="work", bufs=3))
+        outp = ctx.enter_context(tc.tile_pool(name="outp", bufs=OBUFS))
+        psum = ctx.enter_context(tc.psum_pool(name="psum", bufs=1))
+        ctx.enter_context(tc.manual_schedule())
+
+        def bank(tag):
+            return psum.tile([P, 512], F32, name=tag, tag=tag)
+
+        scr = const.tile([P, 8], F32, name="scr")
+        scr2 = const.tile([P, 8], F32, name="scr2")
+        ones = const.tile([P, P], BF16, name="ones")
+        braw = const.tile([P, HDIM], BF16, name="braw")
+        ident = const.tile([P, P], F32, name="ident")
+        nc.vector.memset(scr[:], 0.0)
+        nc.vector.memset(braw[:], 0.0)
+        nc.vector.memset(ones[:], 1.0)
+        nc.scalar.activation(out=scr2[:], in_=scr[:], func=SIGMOID)
+        masks.make_identity(nc, ident[:])
+        for r, bvec in enumerate((bi, bh, b0, b1)):
+            nc.scalar.dma_start(out=braw[r : r + 1, :], in_=bvec.rearrange("(o h) -> o h", o=1))
+
+        where = {}
+        first_tile = []
+        t0 = 0
+        for n in CHUNKS:
+            first_tile.append(t0)
+            t0 += n
+
+        def load_chunk(c):
+            n = CHUNKS[c]
+            a = first_tile[c]
+            s_t = inp.tile([P, n, SK], BF16, name="s%d" % c)
+            xt = inp.tile([P, n, IDIM], BF16, name="x%d" % c)
+            ht = inp.tile([P, n, HDIM], BF16, name="h%d" % c)
+            nc.sync.dma_start(out=s_t[:], in_=s_v[:, a : a + n, :])
+            nc.sync.dma_start(out=xt[:], in_=x_v[:, a : a + n, :])
+            nc.sync.dma_start(out=ht[:], in_=h_v[:, a : a + n, :])
+            for j in range(n):
+                where[a + j] = (xt, ht, s_t, j)
+
+        w01_raw = const.tile([P, 4, SK], BF16, name="w01_raw")
+        wi_raw = const.tile([P, 4, IDIM], BF16, name="wi_raw")
+        wh_raw = const.tile([P, 4, HDIM], BF16, name="wh_raw")
+        load_chunk(0)
+        nc.sync.dma_start(out=w01_raw[:, :, 0:128], in_=W0.rearrange("(a p) k -> p a k", p=P))
+        nc.sync.dma_start(out=w01_raw[:, :, 128:256], in_=W1.rearrange("(a p) k -> p a k", p=P))
+        wi_v = Wi.rearrange("(a p) k -> p a k", p=P)
+        for a in range(4):
+            nc.sync.dma_start(out=wi_raw[:, a, :], in_=wi_v[:, a, :])
+        nc.sync.dma_start(out=wh_raw[:], in_=Wh.rearrange("(a p) k -> p a k", p=P))
+        loaded = 1
+        for c in range(1, len(CHUNKS)):
+            if first_tile[c] // G <= LOOKAHEAD:
+                load_chunk(c)
+                loaded = c + 1
+
+        st = {}
+
+        def t_list(i):
+            ts_b, th_b = bank("ts"), bank("th")
+            tx_b = [bank("tx0"), bank("tx1")]
+            st["ts", i], st["th", i], st["tx", i] = ts_b, th_b, tx_b
+            ops = []
+            for j in range(G):
+                xt, ht, s_t, q = where[G * i + j]
+                ops.append((ts_b[:, 128 * j : 128 * j + 128], s_t[:, q, :].bitcast(F32)))
+            for j in range(G):
+                xt, ht, s_t, q = where[G * i + j]
+                src = xt[:, q, :].bitcast(F32)
+                for w in range(4):
+                    g, u = w // 2, w % 2
+                    ops.append((tx_b[j][:, 128 * w : 128 * w + 128], src[:, 256 * g + u : 256 * g + 256 : 2]))
+            for j in range(G):
+                xt, ht, s_t, q = where[G * i + j]
+                src = ht[:, q, :].bitcast(F32)
+                for u in range(2):
+                    c = 128 * (2 * j + u)
+                    ops.append((th_b[:, c : c + 128], src[:, u:256:2]))
+            return ops
+
+        def do_t(op):
+            nc.tensor.transpose(op[0], op[1], ident[:])
+
+        def copies(i):
+            sg = work.tile([P, 512], BF16, name="sg", tag="sg")
+            xg = work.tile([P, 2048], BF16, name="xg", tag="xg", align_bytes=64)
+            hg = work.tile([P, 1024], BF16, name="hg", tag="hg", align_bytes=64)
+            st["sg", i], st["xg", i], st["hg", i] = sg, xg, hg
+            nc.scalar.copy(out=sg[:].bitcast(F32), in_=st["ts", i][:, 0:256])
+            for j in range(G):
+                nc.scalar.copy(
+                    out=xg[:, 1024 * j : 1024 * j + 1024].bitcast(F32).rearrange("p (g b u) -> p g b u", g=2, u=2),
+                    in_=st["tx", i][j][:].rearrange("p (g u b) -> p g b u", g=2, u=2),
+                )
+            nc.scalar.copy(
+                out=hg[:].bitcast(F32).rearrange("p (j b u) -> p j b u", j=2, u=2),
+                in_=st["th", i][:].rearrange("p (j u b) -> p j b u", j=2, u=2),
+            )
+
+        def quantise(i):
+            xc = work.tile([P, 512], U32, name="xc", tag="xc", align_bytes=64)
+            xs = work.tile([P, 512], U8, name="xs", tag="xs", align_bytes=64)
+            hc = work.tile([P, 256], U32, name="hc", tag="hc", align_bytes=64)
+            hs = work.tile([P, 256], U8, name="hs", tag="hs", align_bytes=64)
+            st["xc", i], st["xs", i], st["hc", i], st["hs", i] = xc, xs, hc, hs
+            nc.vector.quantize_mx(out=xc[:].bitcast(FP8X4), scales=xs[:], in_=st["xg", i][:])
+            nc.vector.quantize_mx(out=hc[:].bitcast(FP8X4), scales=hs[:], in_=st["hg", i][:])
+
+        def p_list(i):
+            pp = [bank("pp0"), bank("pp1")]
+            st["pp", i] = pp
+            sgv = st["sg", i][:].rearrange("p (j b e) -> p j b e", j=2, e=2)
+            ops = []
+            for j in range(G):
+                for e in range(2):
+                    ops.append((pp[j], sgv[:, j, :, e], e))
+            return ops
+
+        def do_p(op):
+            nc.tensor.matmul(op[0][:], lhsT=op[1], rhs=w01[:, op[2], :], start=(op[2] == 0), stop=(op[2] == 1))
+
+        def weave(plains, trans):
+            k = 0
+            for op in plains:
+                do_p(op)
+                for tr in trans[k : k + WEAVE]:
+                    do_t(tr)
+                k += WEAVE
+            for tr in trans[k:]:
+                do_t(tr)
+
+        def mx(i):
+            pm = [bank("pm0"), bank("pm1")]
+            st["pm", i] = pm
+            xc, xs, hc, hs = st["xc", i], st["xs", i], st["hc", i], st["hs", i]
+            for j in range(G):
+                for g in range(2):
+                    c = 128 * (2 * j + g)
+                    nc.tensor.matmul_mx(
+                        out=pm[j][:],
+                        lhsT=xc[:, c : c + 128].bitcast(FP8X4),
+                        lhsT_scale=xs[:, c : c + 128],
+                        rhs=wic[:, 512 * g : 512 * g + 512].bitcast(FP8X4),
+                        rhs_scale=wis[:, 512 * g : 512 * g + 512],
+                        start=(g == 0),
+                        stop=False,
+                    )
+                c = 128 * j
+                nc.tensor.matmul_mx(
+                    out=pm[j][:],
+                    lhsT=hc[:, c : c + 128].bitcast(FP8X4),
+                    lhsT_scale=hs[:, c : c + 128],
+                    rhs=whc[:].bitcast(FP8X4),
+                    rhs_scale=whs[:],
+                    start=False,
+                    stop=True,
+                )
+
+        def e1(i):
+            o = outp.tile([P, G, HDIM], F32, name="o", tag="o")
+            st["o", i] = o
+            for j in range(G):
+                nc.vector.tensor_tensor(out=o[:, j, :], in0=st["pp", i][j][:], in1=bias[:], op=ADD)
+
+        def e2(i):
+            o = st["o", i]
+            for j in range(G):
+                nc.vector.tensor_tensor(out=o[:, j, :], in0=st["pm", i][j][:], in1=o[:, j, :], op=ADD)
+
+        def e3(i):
+            o = st["o", i]
+            flat = o[:].rearrange("p j h -> p (j h)")
+            nc.scalar.activation(out=flat, in_=flat, func=SIGMOID)
+            nc.sync.dma_start(out=o_v[:, G * i : G * i + G, :], in_=o[:])
+
+        def last_epilogue(i):
+            o = st["o", i]
+            for j, lo, hi in ((0, 0, 512), (1, 0, 256), (1, 256, 512)):
+                piece = o[:, j, lo:hi]
+                nc.vector.tensor_tensor(out=piece, in0=st["pm", i][j][:, lo:hi], in1=piece, op=ADD)
+                nc.scalar.activation(out=piece, in_=piece, func=SIGMOID)
+                nc.sync.dma_start(out=o_v[:, G * i + j, lo:hi], in_=piece)
+
+        w01 = const.tile([P, 2, HDIM], BF16, name="w01")
+        bias = const.tile([P, HDIM], F32, name="bias")
+        wig = const.tile([P, 4096], BF16, name="wig", align_bytes=64)
+        whg = const.tile([P, 2048], BF16, name="whg", align_bytes=64)
+        wic = const.tile([P, 1024], U32, name="wic", align_bytes=64)
+        wis = const.tile([P, 1024], U8, name="wis", align_bytes=64)
+        whc = const.tile([P, 512], U32, name="whc", align_bytes=64)
+        whs = const.tile([P, 512], U8, name="whs", align_bytes=64)
+
+        for op in t_list(0):
+            do_t(op)
+        copies(0)
+        w01_b = [bank("pm0"), bank("pm1")]
+        for a in range(4):
+            c = 128 * (a % 2)
+            do_t((w01_b[a // 2][:, c : c + 128], w01_raw[:, a, :].bitcast(F32)))
+        for r, eng_copy in enumerate((nc.scalar.copy, nc.vector.tensor_copy)):
+            eng_copy(
+                out=w01[:, :, 256 * r : 256 * r + 256],
+                in_=w01_b[r][:, 0:256].bitcast(BF16).rearrange("p (h e) -> p e h", e=2),
+            )
+        quantise(0)
+        wi_banks = [bank("tx0"), bank("tx1"), bank("th"), bank("ts")]
+        wi_ops = []
+        for a in range(4):
+            src = wi_raw[:, a, :].bitcast(F32)
+            for w in range(4):
+                g, u = w // 2, w % 2
+                wi_ops.append((wi_banks[a][:, 128 * w : 128 * w + 128], src[:, 256 * g + u : 256 * g + 256 : 2]))
+        weave(p_list(0), wi_ops)
+        wig_v = wig[:].bitcast(F32).rearrange("p (g h u) -> p g h u", g=2, u=2)
+        for a in range(4):
+            dst = wig_v[:, :, 128 * a : 128 * a + 128, :]
+            src = wi_banks[a][:].rearrange("p (g u h) -> p g h u", g=2, u=2)
+            if a % 2 == 0:
+                nc.scalar.copy(out=dst, in_=src)
+            else:
+                nc.vector.tensor_copy(out=dst, in_=src)
+        bias_b = bank("tx0")
+        nc.tensor.matmul(bias_b[:], lhsT=ones[:], rhs=braw[:], start=True, stop=True)
+        nc.vector.tensor_copy(out=bias[:], in_=bias_b[:])
+        for g in range(2):
+            nc.vector.quantize_mx(
+                out=wic[:, 512 * g : 512 * g + 512].bitcast(FP8X4),
+                scales=wis[:, 512 * g : 512 * g + 512],
+                in_=wig[:, 2048 * g : 2048 * g + 2048],
+            )
+        wh_banks = [bank("pm0"), bank("pm1")]
+        for a in range(4):
+            src = wh_raw[:, a, :].bitcast(F32)
+            for u in range(2):
+                c = 128 * (2 * (a % 2) + u)
+                do_t((wh_banks[a // 2][:, c : c + 128], src[:, u:256:2]))
+        whg_v = whg[:].bitcast(F32).rearrange("p (r a h u) -> p r a h u", r=2, a=2, u=2)
+        for r in range(2):
+            nc.scalar.copy(out=whg_v[:, r], in_=wh_banks[r][:].rearrange("p (a u h) -> p a h u", a=2, u=2))
+        nc.vector.quantize_mx(out=whc[:].bitcast(FP8X4), scales=whs[:], in_=whg[:])
+        e1(0)
+
+        for i in range(1, NG + 1):
+            while loaded < len(CHUNKS) and first_tile[loaded] // G <= i + LOOKAHEAD:
+                load_chunk(loaded)
+                loaded += 1
+            plains = p_list(i - 1) if 2 <= i <= NG else []
+            trans = t_list(i) if i < NG else []
+            weave(plains, trans)
+            if i < NG:
+                copies(i)
+            if 2 <= i <= NG:
+                e1(i - 1)
+            mx(i - 1)
+            if i < NG:
+                quantise(i)
+            if i >= 2:
+                e3(i - 2)
+            if i < NG:
+                e2(i - 1)
+            else:
+                last_epilogue(i - 1)

@@ -35,6 +35,7 @@ def tile_stackrnn_pa_t_kernel(tc, x, hidden, stack_top, Wi, bi, Wh, bh, W0, b0, 
         const = ctx.enter_context(tc.tile_pool(name="const", bufs=1))
         inp = ctx.enter_context(tc.tile_pool(name="inp", bufs=1))
         work = ctx.enter_context(tc.tile_pool(name="work", bufs=3))
+        ahead = ctx.enter_context(tc.tile_pool(name="ahead", bufs=3))
         outp = ctx.enter_context(tc.tile_pool(name="outp", bufs=OBUFS))
         psum = ctx.enter_context(tc.psum_pool(name="psum", bufs=1))
         ctx.enter_context(tc.manual_schedule())
@@ -102,17 +103,41 @@ def tile_stackrnn_pa_t_kernel(tc, x, hidden, stack_top, Wi, bi, Wh, bh, W0, b0, 
                 ops.append((ts_b[:, 128 * j : 128 * j + 128], s_t[:, q, :].bitcast(F32)))
             for j in range(G):
                 xt, ht, s_t, q = where[G * i + j]
-                src = xt[:, q, :].bitcast(F32)
                 for w in range(4):
-                    g, u = w // 2, w % 2
-                    ops.append((tx_b[j][:, 128 * w : 128 * w + 128], src[:, 256 * g + u : 256 * g + 256 : 2]))
+                    if ("xq", i) in st:
+                        src = st["xq", i][:, j, 256 * w : 256 * w + 256].bitcast(F32)
+                    else:
+                        g, u = w // 2, w % 2
+                        src = xt[:, q, :].bitcast(F32)[:, 256 * g + u : 256 * g + 256 : 2]
+                    ops.append((tx_b[j][:, 128 * w : 128 * w + 128], src))
             for j in range(G):
                 xt, ht, s_t, q = where[G * i + j]
-                src = ht[:, q, :].bitcast(F32)
                 for u in range(2):
+                    if ("hq", i) in st:
+                        src = st["hq", i][:, j, 256 * u : 256 * u + 256].bitcast(F32)
+                    else:
+                        src = ht[:, q, :].bitcast(F32)[:, u:256:2]
                     c = 128 * (2 * j + u)
-                    ops.append((th_b[:, c : c + 128], src[:, u:256:2]))
+                    ops.append((th_b[:, c : c + 128], src))
             return ops
+
+        def split(dst, src):
+            nc.gpsimd.tensor_copy(
+                out=dst.bitcast(F32).rearrange("p (u b) -> p u b", u=2),
+                in_=src.bitcast(F32).rearrange("p (b u) -> p u b", u=2),
+            )
+
+        def permute(i):
+            xq = ahead.tile([P, G, IDIM], BF16, name="xq", tag="xq", align_bytes=64)
+            hq = ahead.tile([P, G, HDIM], BF16, name="hq", tag="hq", align_bytes=64)
+            st["xq", i], st["hq", i] = xq, hq
+            for j in range(G):
+                xt, ht, s_t, q = where[G * i + j]
+                for c in range(0, IDIM, 512):
+                    split(xq[:, j, c : c + 512], xt[:, q, c : c + 512])
+            for j in range(G):
+                xt, ht, s_t, q = where[G * i + j]
+                split(hq[:, j, :], ht[:, q, :])
 
         def do_t(op):
             nc.tensor.transpose(op[0], op[1], ident[:])
@@ -280,6 +305,9 @@ def tile_stackrnn_pa_t_kernel(tc, x, hidden, stack_top, Wi, bi, Wh, bh, W0, b0, 
             while loaded < len(CHUNKS) and first_tile[loaded] // G <= i + LOOKAHEAD:
                 load_chunk(loaded)
                 loaded += 1
+            for n in (2, 3) if i == 1 else (i + 2,):
+                if n < NG:
+                    permute(n)
             plains = p_list(i - 1) if 2 <= i <= NG else []
             trans = t_list(i) if i < NG else []
             weave(plains, trans)

@@ -104,40 +104,31 @@ def tile_stackrnn_pa_t_kernel(tc, x, hidden, stack_top, Wi, bi, Wh, bh, W0, b0, 
             for j in range(G):
                 xt, ht, s_t, q = where[G * i + j]
                 for w in range(4):
-                    if ("xq", i) in st:
-                        src = st["xq", i][:, j, 256 * w : 256 * w + 256].bitcast(F32)
-                    else:
-                        g, u = w // 2, w % 2
-                        src = xt[:, q, :].bitcast(F32)[:, 256 * g + u : 256 * g + 256 : 2]
+                    src = st["xq", i][:, j, 256 * w : 256 * w + 256].bitcast(F32)
                     ops.append((tx_b[j][:, 128 * w : 128 * w + 128], src))
             for j in range(G):
                 xt, ht, s_t, q = where[G * i + j]
                 for u in range(2):
-                    if ("hq", i) in st:
-                        src = st["hq", i][:, j, 256 * u : 256 * u + 256].bitcast(F32)
-                    else:
-                        src = ht[:, q, :].bitcast(F32)[:, u:256:2]
+                    src = st["hq", i][:, j, 256 * u : 256 * u + 256].bitcast(F32)
                     c = 128 * (2 * j + u)
                     ops.append((th_b[:, c : c + 128], src))
             return ops
 
-        def split(dst, src):
-            nc.gpsimd.tensor_copy(
-                out=dst.bitcast(F32).rearrange("p (u b) -> p u b", u=2),
-                in_=src.bitcast(F32).rearrange("p (b u) -> p u b", u=2),
-            )
+        def split(eng, dst, src):
+            d = dst.rearrange("p j k -> p (j k)").bitcast(F32).rearrange("p (m v q e) -> p m v q e", v=2, q=16, e=8)
+            s = src.rearrange("p j k -> p (j k)").bitcast(F32).rearrange("p (m q v e) -> p m q v e", q=16, v=2, e=8)
+            for v in range(2):
+                eng.tensor_copy(out=d[:, :, v, :, :], in_=s[:, :, :, v, :])
 
-        def permute(i):
-            xq = ahead.tile([P, G, IDIM], BF16, name="xq", tag="xq", align_bytes=64)
-            hq = ahead.tile([P, G, HDIM], BF16, name="hq", tag="hq", align_bytes=64)
-            st["xq", i], st["hq", i] = xq, hq
-            for j in range(G):
-                xt, ht, s_t, q = where[G * i + j]
-                for c in range(0, IDIM, 512):
-                    split(xq[:, j, c : c + 512], xt[:, q, c : c + 512])
-            for j in range(G):
-                xt, ht, s_t, q = where[G * i + j]
-                split(hq[:, j, :], ht[:, q, :])
+        def split_pair(eng, src, tag, width):
+            dst = ahead.tile([P, G, width], BF16, name=tag, tag=tag, align_bytes=64)
+            split(eng, dst[:], src)
+            return dst
+
+        def permute(eng, i):
+            xt, ht, s_t, q = where[G * i]
+            st["xq", i] = split_pair(eng, xt[:, q : q + G, :], "xq", IDIM)
+            st["hq", i] = split_pair(eng, ht[:, q : q + G, :], "hq", HDIM)
 
         def do_t(op):
             nc.tensor.transpose(op[0], op[1], ident[:])
@@ -251,6 +242,7 @@ def tile_stackrnn_pa_t_kernel(tc, x, hidden, stack_top, Wi, bi, Wh, bh, W0, b0, 
         whc = const.tile([P, 512], U32, name="whc", align_bytes=64)
         whs = const.tile([P, 512], U8, name="whs", align_bytes=64)
 
+        permute(nc.vector, 0)
         for op in t_list(0):
             do_t(op)
         copies(0)
@@ -263,14 +255,16 @@ def tile_stackrnn_pa_t_kernel(tc, x, hidden, stack_top, Wi, bi, Wh, bh, W0, b0, 
                 out=w01[:, :, 256 * r : 256 * r + 256],
                 in_=w01_b[r][:, 0:256].bitcast(BF16).rearrange("p (h e) -> p e h", e=2),
             )
+        wiq = [split_pair(nc.vector, wi_raw[:, a : a + 2, :], "xq", IDIM) for a in (0, 2)]
         quantise(0)
+        whq = [split_pair(nc.vector, wh_raw[:, a : a + 2, :], "hq", HDIM) for a in (0, 2)]
+        permute(nc.gpsimd, 1)
         wi_banks = [bank("tx0"), bank("tx1"), bank("th"), bank("ts")]
         wi_ops = []
         for a in range(4):
-            src = wi_raw[:, a, :].bitcast(F32)
+            src = wiq[a // 2][:, a % 2, :].bitcast(F32)
             for w in range(4):
-                g, u = w // 2, w % 2
-                wi_ops.append((wi_banks[a][:, 128 * w : 128 * w + 128], src[:, 256 * g + u : 256 * g + 256 : 2]))
+                wi_ops.append((wi_banks[a][:, 128 * w : 128 * w + 128], src[:, 128 * w : 128 * w + 128]))
         weave(p_list(0), wi_ops)
         wig_v = wig[:].bitcast(F32).rearrange("p (g h u) -> p g h u", g=2, u=2)
         for a in range(4):
@@ -291,10 +285,10 @@ def tile_stackrnn_pa_t_kernel(tc, x, hidden, stack_top, Wi, bi, Wh, bh, W0, b0, 
             )
         wh_banks = [bank("pm0"), bank("pm1")]
         for a in range(4):
-            src = wh_raw[:, a, :].bitcast(F32)
+            src = whq[a // 2][:, a % 2, :].bitcast(F32)
             for u in range(2):
                 c = 128 * (2 * (a % 2) + u)
-                do_t((wh_banks[a // 2][:, c : c + 128], src[:, u:256:2]))
+                do_t((wh_banks[a // 2][:, c : c + 128], src[:, 128 * u : 128 * u + 128]))
         whg_v = whg[:].bitcast(F32).rearrange("p (r a h u) -> p r a h u", r=2, a=2, u=2)
         for r in range(2):
             nc.scalar.copy(out=whg_v[:, r], in_=wh_banks[r][:].rearrange("p (a u h) -> p a h u", a=2, u=2))
@@ -307,7 +301,7 @@ def tile_stackrnn_pa_t_kernel(tc, x, hidden, stack_top, Wi, bi, Wh, bh, W0, b0, 
                 loaded += 1
             for n in (2, 3) if i == 1 else (i + 2,):
                 if n < NG:
-                    permute(n)
+                    permute(nc.gpsimd, n)
             plains = p_list(i - 1) if 2 <= i <= NG else []
             trans = t_list(i) if i < NG else []
             weave(plains, trans)

@@ -97,22 +97,17 @@ def tile_stackrnn_pa_t_kernel(tc, x, hidden, stack_top, Wi, bi, Wh, bh, W0, b0, 
             ts_b, th_b = bank("ts"), bank("th")
             tx_b = [bank("tx0"), bank("tx1")]
             st["ts", i], st["th", i], st["tx", i] = ts_b, th_b, tx_b
-            ops = []
+            stack, hid, xs = [], [], []
             for j in range(G):
                 xt, ht, s_t, q = where[G * i + j]
-                ops.append((ts_b[:, 128 * j : 128 * j + 128], s_t[:, q, :].bitcast(F32)))
-            for j in range(G):
-                xt, ht, s_t, q = where[G * i + j]
+                stack.append((ts_b[:, 128 * j : 128 * j + 128], s_t[:, q, :].bitcast(F32)))
+                for u in range(2):
+                    col = 128 * (2 * j + u)
+                    hid.append((th_b[:, col : col + 128], ht[:, q, :].bitcast(F32)[:, u:256:2]))
                 for w in range(4):
                     src = st["xq", i][:, j, 256 * w : 256 * w + 256].bitcast(F32)
-                    ops.append((tx_b[j][:, 128 * w : 128 * w + 128], src))
-            for j in range(G):
-                xt, ht, s_t, q = where[G * i + j]
-                for u in range(2):
-                    src = st["hq", i][:, j, 256 * u : 256 * u + 256].bitcast(F32)
-                    c = 128 * (2 * j + u)
-                    ops.append((th_b[:, c : c + 128], src))
-            return ops
+                    xs.append((tx_b[j][:, 128 * w : 128 * w + 128], src))
+            return [hid[0], stack[0], hid[1], stack[1], hid[2], xs[0], hid[3]] + xs[1:]
 
         def split(eng, dst, src):
             d = dst.rearrange("p j k -> p (j k)").bitcast(F32).rearrange("p (m v q e) -> p m v q e", v=2, q=16, e=8)
@@ -120,15 +115,16 @@ def tile_stackrnn_pa_t_kernel(tc, x, hidden, stack_top, Wi, bi, Wh, bh, W0, b0, 
             for v in range(2):
                 eng.tensor_copy(out=d[:, :, v, :, :], in_=s[:, :, :, v, :])
 
-        def split_pair(eng, src, tag, width):
-            dst = ahead.tile([P, G, width], BF16, name=tag, tag=tag, align_bytes=64)
-            split(eng, dst[:], src)
+        def split_pair(eng, src, parts):
+            dst = ahead.tile([P, G, IDIM], BF16, name="xq", tag="xq", align_bytes=64)
+            n = G // parts
+            for j in range(0, G, n):
+                split(eng, dst[:, j : j + n, :], src[:, j : j + n, :])
             return dst
 
-        def permute(eng, i):
+        def permute(eng, i, parts):
             xt, ht, s_t, q = where[G * i]
-            st["xq", i] = split_pair(eng, xt[:, q : q + G, :], "xq", IDIM)
-            st["hq", i] = split_pair(eng, ht[:, q : q + G, :], "hq", HDIM)
+            st["xq", i] = split_pair(eng, xt[:, q : q + G, :], parts)
 
         def do_t(op):
             nc.tensor.transpose(op[0], op[1], ident[:])
@@ -139,15 +135,15 @@ def tile_stackrnn_pa_t_kernel(tc, x, hidden, stack_top, Wi, bi, Wh, bh, W0, b0, 
             hg = work.tile([P, 1024], BF16, name="hg", tag="hg", align_bytes=64)
             st["sg", i], st["xg", i], st["hg", i] = sg, xg, hg
             nc.scalar.copy(out=sg[:].bitcast(F32), in_=st["ts", i][:, 0:256])
+            nc.scalar.copy(
+                out=hg[:].bitcast(F32).rearrange("p (j b u) -> p j b u", j=2, u=2),
+                in_=st["th", i][:].rearrange("p (j u b) -> p j b u", j=2, u=2),
+            )
             for j in range(G):
                 nc.scalar.copy(
                     out=xg[:, 1024 * j : 1024 * j + 1024].bitcast(F32).rearrange("p (g b u) -> p g b u", g=2, u=2),
                     in_=st["tx", i][j][:].rearrange("p (g u b) -> p g b u", g=2, u=2),
                 )
-            nc.scalar.copy(
-                out=hg[:].bitcast(F32).rearrange("p (j b u) -> p j b u", j=2, u=2),
-                in_=st["th", i][:].rearrange("p (j u b) -> p j b u", j=2, u=2),
-            )
 
         def quantise(i):
             xc = work.tile([P, 512], U32, name="xc", tag="xc", align_bytes=64)
@@ -155,8 +151,8 @@ def tile_stackrnn_pa_t_kernel(tc, x, hidden, stack_top, Wi, bi, Wh, bh, W0, b0, 
             hc = work.tile([P, 256], U32, name="hc", tag="hc", align_bytes=64)
             hs = work.tile([P, 256], U8, name="hs", tag="hs", align_bytes=64)
             st["xc", i], st["xs", i], st["hc", i], st["hs", i] = xc, xs, hc, hs
-            nc.vector.quantize_mx(out=xc[:].bitcast(FP8X4), scales=xs[:], in_=st["xg", i][:])
             nc.vector.quantize_mx(out=hc[:].bitcast(FP8X4), scales=hs[:], in_=st["hg", i][:])
+            nc.vector.quantize_mx(out=xc[:].bitcast(FP8X4), scales=xs[:], in_=st["xg", i][:])
 
         def p_list(i):
             pp = [bank("pp0"), bank("pp1")]
@@ -242,7 +238,7 @@ def tile_stackrnn_pa_t_kernel(tc, x, hidden, stack_top, Wi, bi, Wh, bh, W0, b0, 
         whc = const.tile([P, 512], U32, name="whc", align_bytes=64)
         whs = const.tile([P, 512], U8, name="whs", align_bytes=64)
 
-        permute(nc.vector, 0)
+        permute(nc.vector, 0, 1)
         for op in t_list(0):
             do_t(op)
         copies(0)
@@ -255,10 +251,9 @@ def tile_stackrnn_pa_t_kernel(tc, x, hidden, stack_top, Wi, bi, Wh, bh, W0, b0, 
                 out=w01[:, :, 256 * r : 256 * r + 256],
                 in_=w01_b[r][:, 0:256].bitcast(BF16).rearrange("p (h e) -> p e h", e=2),
             )
-        wiq = [split_pair(nc.vector, wi_raw[:, a : a + 2, :], "xq", IDIM) for a in (0, 2)]
+        wiq = [split_pair(nc.vector, wi_raw[:, a : a + 2, :], 1) for a in (0, 2)]
         quantise(0)
-        whq = [split_pair(nc.vector, wh_raw[:, a : a + 2, :], "hq", HDIM) for a in (0, 2)]
-        permute(nc.gpsimd, 1)
+        permute(nc.gpsimd, 1, 2)
         wi_banks = [bank("tx0"), bank("tx1"), bank("th"), bank("ts")]
         wi_ops = []
         for a in range(4):
@@ -285,10 +280,10 @@ def tile_stackrnn_pa_t_kernel(tc, x, hidden, stack_top, Wi, bi, Wh, bh, W0, b0, 
             )
         wh_banks = [bank("pm0"), bank("pm1")]
         for a in range(4):
-            src = whq[a // 2][:, a % 2, :].bitcast(F32)
+            src = wh_raw[:, a, :].bitcast(F32)
             for u in range(2):
                 c = 128 * (2 * (a % 2) + u)
-                do_t((wh_banks[a // 2][:, c : c + 128], src[:, 128 * u : 128 * u + 128]))
+                do_t((wh_banks[a // 2][:, c : c + 128], src[:, u:256:2]))
         whg_v = whg[:].bitcast(F32).rearrange("p (r a h u) -> p r a h u", r=2, a=2, u=2)
         for r in range(2):
             nc.scalar.copy(out=whg_v[:, r], in_=wh_banks[r][:].rearrange("p (a u h) -> p a h u", a=2, u=2))
@@ -301,7 +296,7 @@ def tile_stackrnn_pa_t_kernel(tc, x, hidden, stack_top, Wi, bi, Wh, bh, W0, b0, 
                 loaded += 1
             for n in (2, 3) if i == 1 else (i + 2,):
                 if n < NG:
-                    permute(nc.gpsimd, n)
+                    permute(nc.gpsimd, n, 2)
             plains = p_list(i - 1) if 2 <= i <= NG else []
             trans = t_list(i) if i < NG else []
             weave(plains, trans)

@@ -35,7 +35,7 @@ def tile_stackrnn_pa_t_kernel(tc, x, hidden, stack_top, Wi, bi, Wh, bh, W0, b0, 
         const = ctx.enter_context(tc.tile_pool(name="const", bufs=1))
         inp = ctx.enter_context(tc.tile_pool(name="inp", bufs=1))
         work = ctx.enter_context(tc.tile_pool(name="work", bufs=3))
-        ahead = ctx.enter_context(tc.tile_pool(name="ahead", bufs=3))
+        once = ctx.enter_context(tc.tile_pool(name="once", bufs=1))
         outp = ctx.enter_context(tc.tile_pool(name="outp", bufs=OBUFS))
         psum = ctx.enter_context(tc.psum_pool(name="psum", bufs=1))
         ctx.enter_context(tc.manual_schedule())
@@ -115,23 +115,23 @@ def tile_stackrnn_pa_t_kernel(tc, x, hidden, stack_top, Wi, bi, Wh, bh, W0, b0, 
             for v in range(2):
                 eng.tensor_copy(out=d[:, :, v, :, :], in_=s[:, :, :, v, :])
 
-        def split_pair(eng, src, parts):
-            dst = ahead.tile([P, G, IDIM], BF16, name="xq", tag="xq", align_bytes=64)
-            n = G // parts
-            for j in range(0, G, n):
-                split(eng, dst[:, j : j + n, :], src[:, j : j + n, :])
-            return dst
+        def ring():
+            xr = work.tile([P, 2048], BF16, name="xr", tag="xr", align_bytes=64)
+            return xr
 
-        def permute(eng, i, parts):
+        def permute(i):
             xt, ht, s_t, q = where[G * i]
-            st["xq", i] = split_pair(eng, xt[:, q : q + G, :], parts)
+            xr = ring()
+            st["xq", i] = xr[:].rearrange("p (j k) -> p j k", j=G)
+            for j in range(G):
+                split(nc.gpsimd, st["xq", i][:, j : j + 1, :], xt[:, q + j : q + j + 1, :])
 
         def do_t(op):
             nc.tensor.transpose(op[0], op[1], ident[:])
 
         def copies(i):
             sg = work.tile([P, 512], BF16, name="sg", tag="sg")
-            xg = work.tile([P, 2048], BF16, name="xg", tag="xg", align_bytes=64)
+            xg = ring()
             hg = work.tile([P, 1024], BF16, name="hg", tag="hg", align_bytes=64)
             st["sg", i], st["xg", i], st["hg", i] = sg, xg, hg
             nc.scalar.copy(out=sg[:].bitcast(F32), in_=st["ts", i][:, 0:256])
@@ -238,7 +238,10 @@ def tile_stackrnn_pa_t_kernel(tc, x, hidden, stack_top, Wi, bi, Wh, bh, W0, b0, 
         whc = const.tile([P, 512], U32, name="whc", align_bytes=64)
         whs = const.tile([P, 512], U8, name="whs", align_bytes=64)
 
-        permute(nc.vector, 0, 1)
+        xq0 = once.tile([P, G, IDIM], BF16, name="xq0", align_bytes=64)
+        wiq = once.tile([P, 4, IDIM], BF16, name="wiq", align_bytes=64)
+        st["xq", 0] = xq0
+        split(nc.vector, xq0[:], where[0][0][:])
         for op in t_list(0):
             do_t(op)
         copies(0)
@@ -251,13 +254,14 @@ def tile_stackrnn_pa_t_kernel(tc, x, hidden, stack_top, Wi, bi, Wh, bh, W0, b0, 
                 out=w01[:, :, 256 * r : 256 * r + 256],
                 in_=w01_b[r][:, 0:256].bitcast(BF16).rearrange("p (h e) -> p e h", e=2),
             )
-        wiq = [split_pair(nc.vector, wi_raw[:, a : a + 2, :], 1) for a in (0, 2)]
+        for a in (0, 2):
+            split(nc.vector, wiq[:, a : a + 2, :], wi_raw[:, a : a + 2, :])
         quantise(0)
-        permute(nc.gpsimd, 1, 2)
+        permute(1)
         wi_banks = [bank("tx0"), bank("tx1"), bank("th"), bank("ts")]
         wi_ops = []
         for a in range(4):
-            src = wiq[a // 2][:, a % 2, :].bitcast(F32)
+            src = wiq[:, a, :].bitcast(F32)
             for w in range(4):
                 wi_ops.append((wi_banks[a][:, 128 * w : 128 * w + 128], src[:, 128 * w : 128 * w + 128]))
         weave(p_list(0), wi_ops)
@@ -294,14 +298,13 @@ def tile_stackrnn_pa_t_kernel(tc, x, hidden, stack_top, Wi, bi, Wh, bh, W0, b0, 
             while loaded < len(CHUNKS) and first_tile[loaded] // G <= i + LOOKAHEAD:
                 load_chunk(loaded)
                 loaded += 1
-            for n in (2, 3) if i == 1 else (i + 2,):
-                if n < NG:
-                    permute(nc.gpsimd, n, 2)
             plains = p_list(i - 1) if 2 <= i <= NG else []
             trans = t_list(i) if i < NG else []
             weave(plains, trans)
             if i < NG:
                 copies(i)
+            if i + 1 < NG:
+                permute(i + 1)
             if 2 <= i <= NG:
                 e1(i - 1)
             mx(i - 1)

from contextlib import ExitStack

import concourse.masks as masks
import concourse.mybir as mybir

F32 = mybir.dt.float32
BF16 = mybir.dt.bfloat16
U32 = mybir.dt.uint32
U8 = mybir.dt.uint8
FP8X4 = mybir.dt.float8_e4m3fn_x4
ADD = mybir.AluOpType.add
SIGMOID = mybir.ActivationFunctionType.Sigmoid

P = 128
B, IDIM, HDIM, SK = 4096, 1024, 512, 256
NT = B // P
G = 2
NG = NT // G
FLOPS = 2 * B * HDIM * (IDIM + HDIM + SK)

CHUNKS = (2, 2, 2, 2, 4, 4, 4, 4, 4, 4)
LOOKAHEAD = 6
WEAVE = 2
OBUFS = 8


def tile_stackrnn_pa_t_kernel(tc, x, hidden, stack_top, Wi, bi, Wh, bh, W0, b0, W1, b1, out):
    nc = tc.nc
    x_v = x.rearrange("(p t) k -> p t k", t=NT)
    h_v = hidden.rearrange("(p t) k -> p t k", t=NT)
    s_v = stack_top.rearrange("(p t) s k -> p t (s k)", t=NT)
    o_v = out.rearrange("(p t) h -> p t h", t=NT)

    with ExitStack() as ctx:
        const = ctx.enter_context(tc.tile_pool(name="const", bufs=1))
        inp = ctx.enter_context(tc.tile_pool(name="inp", bufs=1))
        work = ctx.enter_context(tc.tile_pool(name="work", bufs=3))
        once = ctx.enter_context(tc.tile_pool(name="once", bufs=1))
        outp = ctx.enter_context(tc.tile_pool(name="outp", bufs=OBUFS))
        psum = ctx.enter_context(tc.psum_pool(name="psum", bufs=1))
        ctx.enter_context(tc.manual_schedule())

        def bank(tag):
            return psum.tile([P, 512], F32, name=tag, tag=tag)

        scr = const.tile([P, 8], F32, name="scr")
        scr2 = const.tile([P, 8], F32, name="scr2")
        ones = const.tile([P, P], BF16, name="ones")
        braw = const.tile([P, HDIM], BF16, name="braw")
        ident = const.tile([P, P], F32, name="ident")
        nc.vector.memset(scr[:], 0.0)
        nc.vector.memset(braw[:], 0.0)
        nc.vector.memset(ones[:], 1.0)
        nc.scalar.activation(out=scr2[:], in_=scr[:], func=SIGMOID)
        masks.make_identity(nc, ident[:])
        for r, bvec in enumerate((bi, bh, b0, b1)):
            nc.scalar.dma_start(out=braw[r : r + 1, :], in_=bvec.rearrange("(o h) -> o h", o=1))

        where = {}
        first_tile = []
        t0 = 0
        for n in CHUNKS:
            first_tile.append(t0)
            t0 += n

        def load_chunk(c):
            n = CHUNKS[c]
            a = first_tile[c]
            s_t = inp.tile([P, n, SK], BF16, name="s%d" % c)
            xt = inp.tile([P, n, IDIM], BF16, name="x%d" % c)
            ht = inp.tile([P, n, HDIM], BF16, name="h%d" % c)
            nc.sync.dma_start(out=s_t[:], in_=s_v[:, a : a + n, :])
            nc.sync.dma_start(out=xt[:], in_=x_v[:, a : a + n, :])
            nc.sync.dma_start(out=ht[:], in_=h_v[:, a : a + n, :])
            for j in range(n):
                where[a + j] = (xt, ht, s_t, j)

        w01_raw = const.tile([P, 4, SK], BF16, name="w01_raw")
        wi_raw = const.tile([P, 4, IDIM], BF16, name="wi_raw")
        wh_raw = const.tile([P, 4, HDIM], BF16, name="wh_raw")
        load_chunk(0)
        nc.sync.dma_start(out=w01_raw[:, :, 0:128], in_=W0.rearrange("(a p) k -> p a k", p=P))
        nc.sync.dma_start(out=w01_raw[:, :, 128:256], in_=W1.rearrange("(a p) k -> p a k", p=P))
        wi_v = Wi.rearrange("(a p) k -> p a k", p=P)
        for a in range(4):
            nc.sync.dma_start(out=wi_raw[:, a, :], in_=wi_v[:, a, :])
        nc.sync.dma_start(out=wh_raw[:], in_=Wh.rearrange("(a p) k -> p a k", p=P))
        loaded = 1
        for c in range(1, len(CHUNKS)):
            if first_tile[c] // G <= LOOKAHEAD:
                load_chunk(c)
                loaded = c + 1

        st = {}

        def t_list(i):
            ts_b, th_b = bank("ts"), bank("th")
            tx_b = [bank("tx0"), bank("tx1")]
            st["ts", i], st["th", i], st["tx", i] = ts_b, th_b, tx_b
            stack, hid, xs = [], [], []
            for j in range(G):
                xt, ht, s_t, q = where[G * i + j]
                stack.append((ts_b[:, 128 * j : 128 * j + 128], s_t[:, q, :].bitcast(F32)))
                for u in range(2):
                    col = 128 * (2 * j + u)
                    hid.append((th_b[:, col : col + 128], ht[:, q, :].bitcast(F32)[:, u:256:2]))
                for w in range(4):
                    src = st["xq", i][:, j, 256 * w : 256 * w + 256].bitcast(F32)
                    xs.append((tx_b[j][:, 128 * w : 128 * w + 128], src))
            return [hid[0], stack[0], hid[1], stack[1], hid[2], xs[0], hid[3]] + xs[1:]

        def split(eng, dst, src):
            d = dst.rearrange("p j k -> p (j k)").bitcast(F32).rearrange("p (m v q e) -> p m v q e", v=2, q=16, e=8)
            s = src.rearrange("p j k -> p (j k)").bitcast(F32).rearrange("p (m q v e) -> p m q v e", q=16, v=2, e=8)
            for v in range(2):
                eng.tensor_copy(out=d[:, :, v, :, :], in_=s[:, :, :, v, :])

        def ring():
            xr = work.tile([P, 2048], BF16, name="xr", tag="xr", align_bytes=64)
            return xr

        def permute(i):
            xt, ht, s_t, q = where[G * i]
            xr = ring()
            st["xq", i] = xr[:].rearrange("p (j k) -> p j k", j=G)
            for j in range(G):
                split(nc.gpsimd, st["xq", i][:, j : j + 1, :], xt[:, q + j : q + j + 1, :])

        def do_t(op):
            nc.tensor.transpose(op[0], op[1], ident[:])

        def copies(i):
            sg = work.tile([P, 512], BF16, name="sg", tag="sg")
            xg = ring()
            hg = work.tile([P, 1024], BF16, name="hg", tag="hg", align_bytes=64)
            st["sg", i], st["xg", i], st["hg", i] = sg, xg, hg
            nc.scalar.copy(out=sg[:].bitcast(F32), in_=st["ts", i][:, 0:256])
            nc.scalar.copy(
                out=hg[:].bitcast(F32).rearrange("p (j b u) -> p j b u", j=2, u=2),
                in_=st["th", i][:].rearrange("p (j u b) -> p j b u", j=2, u=2),
            )
            for j in range(G):
                nc.scalar.copy(
                    out=xg[:, 1024 * j : 1024 * j + 1024].bitcast(F32).rearrange("p (g b u) -> p g b u", g=2, u=2),
                    in_=st["tx", i][j][:].rearrange("p (g u b) -> p g b u", g=2, u=2),
                )

        def quantise(i):
            xc = work.tile([P, 512], U32, name="xc", tag="xc", align_bytes=64)
            xs = work.tile([P, 512], U8, name="xs", tag="xs", align_bytes=64)
            hc = work.tile([P, 256], U32, name="hc", tag="hc", align_bytes=64)
            hs = work.tile([P, 256], U8, name="hs", tag="hs", align_bytes=64)
            st["xc", i], st["xs", i], st["hc", i], st["hs", i] = xc, xs, hc, hs
            nc.vector.quantize_mx(out=hc[:].bitcast(FP8X4), scales=hs[:], in_=st["hg", i][:])
            nc.vector.quantize_mx(out=xc[:].bitcast(FP8X4), scales=xs[:], in_=st["xg", i][:])

        def p_list(i):
            pp = [bank("pp0"), bank("pp1")]
            st["pp", i] = pp
            sgv = st["sg", i][:].rearrange("p (j b e) -> p j b e", j=2, e=2)
            ops = []
            for j in range(G):
                for e in range(2):
                    ops.append((pp[j], sgv[:, j, :, e], e))
            return ops

        def do_p(op):
            nc.tensor.matmul(op[0][:], lhsT=op[1], rhs=w01[:, op[2], :], start=(op[2] == 0), stop=(op[2] == 1))

        def weave(plains, trans):
            k = 0
            for op in plains:
                do_p(op)
                for tr in trans[k : k + WEAVE]:
                    do_t(tr)
                k += WEAVE
            for tr in trans[k:]:
                do_t(tr)

        def mx(i):
            pm = [bank("pm0"), bank("pm1")]
            st["pm", i] = pm
            xc, xs, hc, hs = st["xc", i], st["xs", i], st["hc", i], st["hs", i]
            for j in range(G):
                for g in range(2):
                    c = 128 * (2 * j + g)
                    nc.tensor.matmul_mx(
                        out=pm[j][:],
                        lhsT=xc[:, c : c + 128].bitcast(FP8X4),
                        lhsT_scale=xs[:, c : c + 128],
                        rhs=wic[:, 512 * g : 512 * g + 512].bitcast(FP8X4),
                        rhs_scale=wis[:, 512 * g : 512 * g + 512],
                        start=(g == 0),
                        stop=False,
                    )
                c = 128 * j
                nc.tensor.matmul_mx(
                    out=pm[j][:],
                    lhsT=hc[:, c : c + 128].bitcast(FP8X4),
                    lhsT_scale=hs[:, c : c + 128],
                    rhs=whc[:].bitcast(FP8X4),
                    rhs_scale=whs[:],
                    start=False,
                    stop=True,
                )

        def e1(i):
            o = outp.tile([P, G, HDIM], F32, name="o", tag="o")
            st["o", i] = o
            for j in range(G):
                nc.vector.tensor_tensor(out=o[:, j, :], in0=st["pp", i][j][:], in1=bias[:], op=ADD)

        def e2(i):
            o = st["o", i]
            for j in range(G):
                nc.vector.tensor_tensor(out=o[:, j, :], in0=st["pm", i][j][:], in1=o[:, j, :], op=ADD)

        def e3(i):
            o = st["o", i]
            flat = o[:].rearrange("p j h -> p (j h)")
            nc.scalar.activation(out=flat, in_=flat, func=SIGMOID)
            nc.sync.dma_start(out=o_v[:, G * i : G * i + G, :], in_=o[:])

        def last_epilogue(i):
            o = st["o", i]
            for j, lo, hi in ((0, 0, 512), (1, 0, 256), (1, 256, 512)):
                piece = o[:, j, lo:hi]
                nc.vector.tensor_tensor(out=piece, in0=st["pm", i][j][:, lo:hi], in1=piece, op=ADD)
                nc.scalar.activation(out=piece, in_=piece, func=SIGMOID)
                nc.sync.dma_start(out=o_v[:, G * i + j, lo:hi], in_=piece)

        w01 = const.tile([P, 2, HDIM], BF16, name="w01")
        bias = const.tile([P, HDIM], F32, name="bias")
        wig = const.tile([P, 4096], BF16, name="wig", align_bytes=64)
        whg = const.tile([P, 2048], BF16, name="whg", align_bytes=64)
        wic = const.tile([P, 1024], U32, name="wic", align_bytes=64)
        wis = const.tile([P, 1024], U8, name="wis", align_bytes=64)
        whc = const.tile([P, 512], U32, name="whc", align_bytes=64)
        whs = const.tile([P, 512], U8, name="whs", align_bytes=64)

        xq0 = once.tile([P, G, IDIM], BF16, name="xq0", align_bytes=64)
        wiq = once.tile([P, 4, IDIM], BF16, name="wiq", align_bytes=64)
        st["xq", 0] = xq0
        split(nc.vector, xq0[:], where[0][0][:])
        for op in t_list(0):
            do_t(op)
        copies(0)
        w01_b = [bank("pm0"), bank("pm1")]
        for a in range(4):
            c = 128 * (a % 2)
            do_t((w01_b[a // 2][:, c : c + 128], w01_raw[:, a, :].bitcast(F32)))
        for r, eng_copy in enumerate((nc.scalar.copy, nc.vector.tensor_copy)):
            eng_copy(
                out=w01[:, :, 256 * r : 256 * r + 256],
                in_=w01_b[r][:, 0:256].bitcast(BF16).rearrange("p (h e) -> p e h", e=2),
            )
        for a in (0, 2):
            split(nc.vector, wiq[:, a : a + 2, :], wi_raw[:, a : a + 2, :])
        quantise(0)
        permute(1)
        wi_banks = [bank("tx0"), bank("tx1"), bank("th"), bank("ts")]
        wi_ops = []
        for a in range(4):
            src = wiq[:, a, :].bitcast(F32)
            for w in range(4):
                wi_ops.append((wi_banks[a][:, 128 * w : 128 * w + 128], src[:, 128 * w : 128 * w + 128]))
        weave(p_list(0), wi_ops)
        wig_v = wig[:].bitcast(F32).rearrange("p (g h u) -> p g h u", g=2, u=2)
        for a in range(4):
            dst = wig_v[:, :, 128 * a : 128 * a + 128, :]
            src = wi_banks[a][:].rearrange("p (g u h) -> p g h u", g=2, u=2)
            if a % 2 == 0:
                nc.scalar.copy(out=dst, in_=src)
            else:
                nc.vector.tensor_copy(out=dst, in_=src)
        bias_b = bank("tx0")
        nc.tensor.matmul(bias_b[:], lhsT=ones[:], rhs=braw[:], start=True, stop=True)
        nc.vector.tensor_copy(out=bias[:], in_=bias_b[:])
        for g in range(2):
            nc.vector.quantize_mx(
                out=wic[:, 512 * g : 512 * g + 512].bitcast(FP8X4),
                scales=wis[:, 512 * g : 512 * g + 512],
                in_=wig[:, 2048 * g : 2048 * g + 2048],
            )
        wh_banks = [bank("pm0"), bank("pm1")]
        for a in range(4):
            src = wh_raw[:, a, :].bitcast(F32)
            for u in range(2):
                c = 128 * (2 * (a % 2) + u)
                do_t((wh_banks[a // 2][:, c : c + 128], src[:, u:256:2]))
        whg_v = whg[:].bitcast(F32).rearrange("p (r a h u) -> p r a h u", r=2, a=2, u=2)
        for r in range(2):
            nc.scalar.copy(out=whg_v[:, r], in_=wh_banks[r][:].rearrange("p (a u h) -> p a h u", a=2, u=2))
        nc.vector.quantize_mx(out=whc[:].bitcast(FP8X4), scales=whs[:], in_=whg[:])
        e1(0)

        for i in range(1, NG + 1):
            while loaded < len(CHUNKS) and first_tile[loaded] // G <= i + LOOKAHEAD:
                load_chunk(loaded)
                loaded += 1
            plains = p_list(i - 1) if 2 <= i <= NG else []
            trans = t_list(i) if i < NG else []
            weave(plains, trans)
            if i < NG:
                copies(i)
            if i + 1 < NG:
                permute(i + 1)
            if 2 <= i <= NG:
                e1(i - 1)
            mx(i - 1)
            if i < NG:
                quantise(i)
            if i >= 2:
                e3(i - 2)
            if i < NG:
                e2(i - 1)
            else:
                last_epilogue(i - 1)
